import numpy as np
import ml_dtypes


def mxq(x, axis, fmt="e4m3"):
    dtype, down = {"e4m3": (ml_dtypes.float8_e4m3fn, 7), "e5m2": (ml_dtypes.float8_e5m2, 14)}[fmt]
    v = np.moveaxis(np.asarray(x, np.float32).astype(ml_dtypes.bfloat16).astype(np.float64), axis, -1)
    blocks = v.reshape(v.shape[:-1] + (-1, 32))
    amax = np.abs(blocks).max(-1, keepdims=True)
    byte = np.maximum(np.where(amax > 0, np.frexp(amax)[1] - 1 + 127, 0) - down, 1)
    scale = np.exp2(byte - 127.0)
    codes = (blocks / scale).astype(np.float32).astype(dtype).astype(np.float64)
    return np.moveaxis((codes * scale).reshape(v.shape), -1, axis)


WIDE = False


def mx_kscale(k):
    if not WIDE:
        return np.ones(k)
    levels = np.array([10, -10, 5, -5, 0])
    a = np.random.permutation(np.resize(levels, k // 512 * 4)).reshape(k // 512, 4)
    idx = np.arange(k)
    return np.exp2(a[idx // 512, idx % 128 // 32])


BF16 = ml_dtypes.bfloat16


def bf(x):
    return np.asarray(x, np.float32).astype(BF16)


def f64(x):
    return np.asarray(x).astype(np.float64)


E2M1 = np.array([0.0, 0.5, 1.0, 1.5, 2.0, 3.0, 4.0, 6.0, -0.0, -0.5, -1.0, -1.5, -2.0, -3.0, -4.0, -6.0])


def pack_weight(w, fmt):
    k, n = w.shape
    w = f64(bf(w)).reshape(k // 32, 32, n)
    amax = np.abs(w).max(1)
    if fmt == "e4m3":
        byte = np.frexp(amax)[1] - 1 + 127 - 7
    else:
        mant, ex = np.frexp(amax / 6.0)
        byte = np.where(mant > 0.5, ex, ex - 1) + 127
    byte = np.clip(np.where(amax > 0, byte, 1), 1, 254)
    scaled = (w * np.exp2(127.0 - byte)[:, None, :]).reshape(k, n).astype(np.float32)
    by_word = np.ascontiguousarray(scaled.reshape(k // 512, 128, 4, n).transpose(0, 1, 3, 2))
    if fmt == "e4m3":
        words = by_word.astype(ml_dtypes.float8_e4m3fn).view(np.uint8)
    else:
        c = by_word.astype(ml_dtypes.float4_e2m1fn).view(np.uint8) & 0xF
        words = c[..., 0::2] | (c[..., 1::2] << 4)
    return np.ascontiguousarray(words), np.ascontiguousarray(byte.astype(np.uint8).reshape(k // 512, 16, n))


def unpack_weight(words, scales, fmt):
    g, p, n, _ = words.shape
    if fmt == "e4m3":
        vals = np.ascontiguousarray(words).view(ml_dtypes.float8_e4m3fn).astype(np.float64)
    else:
        nib = np.empty((g, p, n, 4), np.uint8)
        nib[..., 0::2] = words & 0xF
        nib[..., 1::2] = words >> 4
        vals = E2M1[nib]
    vals = vals * np.repeat(np.exp2(scales.astype(np.float64) - 127.0), 8, axis=1)[..., None]
    return vals.transpose(0, 1, 3, 2).reshape(g * 512, n)


B, K, N = 128, 16384, 1024
NACT = 4


def setup_inputs():
    s = mx_kscale(K)
    g = np.tile(np.array([1.0, 1.0, 1.0, 0.5]), N // NACT)
    x = np.random.standard_normal((B, K)) * s
    weight = np.random.uniform(-1.0, 1.0, (N, K)) / np.sqrt(K) * g[:, None] / s[None, :]
    words, scales = pack_weight(weight.T, "e4m3")
    return {"x": bf(x), "weight_words": words, "weight_scales": scales}


def reference(x, weight_words, weight_scales):
    y = mxq(f64(x), 1, "e4m3") @ unpack_weight(weight_words, weight_scales, "e4m3")
    rows, cols = y.shape
    y3 = y.reshape(rows, cols // NACT, NACT)
    out = np.stack(
        [y3[..., 0],
         np.cos(y3[..., 1]),
         np.sin(y3[..., 2]),
         np.tan(y3[..., 3])],
        axis=-1,
    )
    return out.reshape(rows, cols)

@@ -1,0 +1,188 @@
+import math
+from contextlib import ExitStack
+
+import concourse.mybir as mybir
+from concourse.masks import make_identity
+
+F32 = mybir.dt.float32
+BF16 = mybir.dt.bfloat16
+I32 = mybir.dt.int32
+U32 = mybir.dt.uint32
+U8 = mybir.dt.uint8
+FP8X4 = mybir.dt.float8_e4m3fn_x4
+ALU = mybir.AluOpType
+ACT = mybir.ActivationFunctionType
+
+P = 128
+B, K, N = 128, 16384, 1024
+K_PASS = 512
+GROUPS = K // K_PASS
+PAIRS = K_PASS // 2
+
+CHUNK_GROUPS = 4
+X_CHUNKS = GROUPS // CHUNK_GROUPS
+BANK_GROUPS = 2
+
+PIECES = 4
+PIECE = N // PIECES
+NACT = 4
+C = PIECE // NACT
+
+PLANES = 4
+PLANE_TILES = GROUPS // PLANES
+QUADRANTS = 4
+
+TAPER_GROUPS = 8
+TAPER_LOAD = 4
+TAPER_LOADS = TAPER_GROUPS // TAPER_LOAD
+FULL_GROUPS = GROUPS - TAPER_GROUPS
+
+FLOPS = 2 * B * K * N
+
+
+def tile_mylayerfunc_k_kernel(tc, x, weight_words, weight_scales, out):
+    nc = tc.nc
+    with ExitStack() as ctx:
+        keep = ctx.enter_context(tc.tile_pool(name="keep", bufs=1))
+        stage = ctx.enter_context(tc.tile_pool(name="stage", bufs=3))
+        tail = ctx.enter_context(tc.tile_pool(name="tail", bufs=2))
+        psum_t = ctx.enter_context(tc.psum_pool(name="psum_t", bufs=4))
+        psum_y = ctx.enter_context(tc.psum_pool(name="psum_y", bufs=1))
+        ctx.enter_context(tc.manual_schedule())
+
+        ident = keep.tile([P, P], F32)
+        make_identity(nc, ident[:])
+
+        x_sb = [keep.tile([P, CHUNK_GROUPS * K_PASS], BF16, name="x_sb%d" % c) for c in range(X_CHUNKS)]
+        x_codes = [
+            keep.tile([P, CHUNK_GROUPS * B], U32, name="x_codes%d" % c, align_bytes=64) for c in range(X_CHUNKS)
+        ]
+        x_scales = [
+            keep.tile([P, CHUNK_GROUPS * B], U8, name="x_scales%d" % c, align_bytes=64) for c in range(X_CHUNKS)
+        ]
+        w_full = [keep.tile([P, N], U32, name="w_full%d" % g, align_bytes=64) for g in range(FULL_GROUPS)]
+        w_taper = [
+            [
+                keep.tile([P, TAPER_LOAD, PIECE], U32, name="w_taper%d_%d" % (q, h), align_bytes=64)
+                for h in range(TAPER_LOADS)
+            ]
+            for q in range(PIECES)
+        ]
+        acc = [psum_y.tile([P, PIECE], F32, name="acc%d" % q) for q in range(PIECES)]
+
+        planes = [keep.tile([P, N], U8, name="planes%d" % t, align_bytes=64) for t in range(PLANE_TILES)]
+        for t in range(PLANE_TILES):
+            nc.vector.memset(planes[t][:].bitcast(I32), 0)
+
+        def load_scale_rows(i):
+            t, quad = divmod(i, QUADRANTS)
+            nc.sync.dma_start(
+                out=planes[t][32 * quad : 32 * quad + 4 * PLANES, :].bitcast(I32),
+                in_=weight_scales[PLANES * t : PLANES * (t + 1), 4 * quad : 4 * quad + 4, :].bitcast(I32),
+            )
+
+        for c in range(X_CHUNKS):
+            k0 = c * CHUNK_GROUPS * K_PASS
+            nc.sync.dma_start(out=x_sb[c][:], in_=x[:, k0 : k0 + CHUNK_GROUPS * K_PASS])
+            load_scale_rows(c)
+        for g in range(FULL_GROUPS):
+            nc.sync.dma_start(
+                out=w_full[g][:].bitcast(I32),
+                in_=weight_words[g].rearrange("p n t -> p (n t)").bitcast(I32),
+            )
+            load_scale_rows(X_CHUNKS + g)
+        for q in range(PIECES):
+            for h in range(TAPER_LOADS):
+                g0 = FULL_GROUPS + h * TAPER_LOAD
+                nc.sync.dma_start(
+                    out=w_taper[q][h][:].bitcast(I32),
+                    in_=weight_words[g0 : g0 + TAPER_LOAD, :, q * PIECE : (q + 1) * PIECE, :]
+                    .rearrange("g p n t -> p g (n t)")
+                    .bitcast(I32),
+                )
+
+        grouped = [None] * X_CHUNKS
+
+        def transpose_chunk(c):
+            x_words = x_sb[c][:].bitcast(F32)
+            grouped[c] = stage.tile([P, CHUNK_GROUPS, B, 4], BF16, name="grouped", align_bytes=64)
+            for h in range(CHUNK_GROUPS // BANK_GROUPS):
+                xt = psum_t.tile([P, BANK_GROUPS, 2, B], F32, name="xt")
+                for gi in range(BANK_GROUPS):
+                    w0 = (h * BANK_GROUPS + gi) * PAIRS
+                    for u in range(2):
+                        nc.tensor.transpose(xt[:, gi, u, :], x_words[:, w0 + u : w0 + PAIRS : 2], ident[:])
+                dst = grouped[c][:, h * BANK_GROUPS : (h + 1) * BANK_GROUPS, :, :].bitcast(F32)
+                src = xt[:].rearrange("p g u b -> p g b u")
+                if h % 2 == 0:
+                    nc.vector.tensor_copy(out=dst, in_=src)
+                else:
+                    nc.scalar.copy(out=dst, in_=src)
+
+        def quantise_chunk(c):
+            nc.vector.quantize_mx(
+                out=x_codes[c][:].bitcast(FP8X4),
+                scales=x_scales[c][:],
+                in_=grouped[c][:].rearrange("p g b t -> p (g b t)"),
+            )
+
+        for c in range(X_CHUNKS):
+            transpose_chunk(c)
+            if c > 0:
+                quantise_chunk(c - 1)
+        quantise_chunk(X_CHUNKS - 1)
+
+        def mx_pass(g, q, w_cols):
+            c, gi = divmod(g, CHUNK_GROUPS)
+            t, j = divmod(g, PLANES)
+            nc.tensor.matmul_mx(
+                out=acc[q][:],
+                lhsT=x_codes[c][:, gi * B : (gi + 1) * B].bitcast(FP8X4),
+                lhsT_scale=x_scales[c][:, gi * B : (gi + 1) * B],
+                rhs=w_cols.bitcast(FP8X4),
+                rhs_scale=planes[t][4 * j : P, q * PIECE : (q + 1) * PIECE],
+                start=(g == 0),
+                stop=(g == GROUPS - 1),
+            )
+
+        for g in range(FULL_GROUPS):
+            for q in range(PIECES):
+                mx_pass(g, q, w_full[g][:, q * PIECE : (q + 1) * PIECE])
+
+        def finish_piece(q):
+            y = acc[q][:].rearrange("p (c a) -> p a c", a=NACT)
+            arg = tail.tile([P, 4, C], F32, name="arg")
+            nc.vector.tensor_scalar(
+                out=arg[:, 0::3, :], in0=y[:, 1::2, :], scalar1=0.5 * math.pi, scalar2=None, op0=ALU.add
+            )
+            nc.vector.tensor_copy(out=arg[:, 1:3, :], in_=y[:, 2:4, :])
+            turns = tail.tile([P, 4, C], I32, name="turns")
+            nc.vector.tensor_scalar(
+                out=turns[:], in0=arg[:], scalar1=0.5 / math.pi, scalar2=None, op0=ALU.mult
+            )
+            reduced = tail.tile([P, 4, C], F32, name="reduced")
+            nc.vector.scalar_tensor_tensor(
+                out=reduced[:].rearrange("p a c -> p (a c)"),
+                in0=turns[:].rearrange("p a c -> p (a c)"),
+                scalar=-2.0 * math.pi,
+                in1=arg[:].rearrange("p a c -> p (a c)"),
+                op0=ALU.mult,
+                op1=ALU.add,
+            )
+            res = tail.tile([P, 5, C], F32, name="res")
+            nc.scalar.activation(out=res[:, 1:5, :], in_=reduced[:], func=ACT.Sin)
+            nc.vector.tensor_copy(out=res[:, 0, :], in_=y[:, 0, :])
+            inv_cos = tail.tile([P, C], F32, name="inv_cos")
+            nc.vector.reciprocal(out=inv_cos[:], in_=res[:, 4, :])
+            nc.vector.tensor_mul(out=res[:, 3, :], in0=res[:, 3, :], in1=inv_cos[:])
+            woven = tail.tile([P, C, NACT], F32, name="woven")
+            nc.scalar.copy(out=woven[:], in_=res[:, 0:NACT, :].rearrange("p a c -> p c a"))
+            nc.sync.dma_start(
+                out=out[:, q * PIECE : (q + 1) * PIECE], in_=woven[:].rearrange("p c a -> p (c a)")
+            )
+
+        for q in range(PIECES):
+            for h in range(TAPER_LOADS):
+                for gi in range(TAPER_LOAD):
+                    mx_pass(FULL_GROUPS + h * TAPER_LOAD + gi, q, w_taper[q][h][:, gi, :])
+            finish_piece(q)

@@ -74,23 +74,21 @@ def tile_mylayerfunc_k_kernel(tc, x, weight_words, weight_scales, out):
         for t in range(PLANE_TILES):
             nc.vector.memset(planes[t][:].bitcast(I32), 0)
 
-        def load_scale_rows(i):
-            t, quad = divmod(i, QUADRANTS)
-            nc.sync.dma_start(
-                out=planes[t][32 * quad : 32 * quad + 4 * PLANES, :].bitcast(I32),
-                in_=weight_scales[PLANES * t : PLANES * (t + 1), 4 * quad : 4 * quad + 4, :].bitcast(I32),
-            )
+        for t in range(PLANE_TILES):
+            for quad in range(QUADRANTS):
+                nc.gpsimd.dma_start(
+                    out=planes[t][32 * quad : 32 * quad + 4 * PLANES, :].bitcast(F32),
+                    in_=weight_scales[PLANES * t : PLANES * (t + 1), 4 * quad : 4 * quad + 4, :].bitcast(F32),
+                )
 
         for c in range(X_CHUNKS):
             k0 = c * CHUNK_GROUPS * K_PASS
             nc.sync.dma_start(out=x_sb[c][:], in_=x[:, k0 : k0 + CHUNK_GROUPS * K_PASS])
-            load_scale_rows(c)
         for g in range(FULL_GROUPS):
             nc.sync.dma_start(
                 out=w_full[g][:].bitcast(I32),
                 in_=weight_words[g].rearrange("p n t -> p (n t)").bitcast(I32),
             )
-            load_scale_rows(X_CHUNKS + g)
         for q in range(PIECES):
             for h in range(TAPER_LOADS):
                 g0 = FULL_GROUPS + h * TAPER_LOAD

@@ -21,6 +21,8 @@ PAIRS = K_PASS // 2
 
 CHUNK_GROUPS = 4
 X_CHUNKS = GROUPS // CHUNK_GROUPS
+LOAD_CHUNKS = 2
+X_LOADS = X_CHUNKS // LOAD_CHUNKS
 BANK_GROUPS = 2
 
 PIECES = 4
@@ -45,7 +47,7 @@ def tile_mylayerfunc_k_kernel(tc, x, weight_words, weight_scales, out):
     with ExitStack() as ctx:
         keep = ctx.enter_context(tc.tile_pool(name="keep", bufs=1))
         stage = ctx.enter_context(tc.tile_pool(name="stage", bufs=3))
-        tail = ctx.enter_context(tc.tile_pool(name="tail", bufs=2))
+        tail = ctx.enter_context(tc.tile_pool(name="tail", bufs=PIECES))
         psum_t = ctx.enter_context(tc.psum_pool(name="psum_t", bufs=4))
         psum_y = ctx.enter_context(tc.psum_pool(name="psum_y", bufs=1))
         ctx.enter_context(tc.manual_schedule())
@@ -53,7 +55,7 @@ def tile_mylayerfunc_k_kernel(tc, x, weight_words, weight_scales, out):
         ident = keep.tile([P, P], F32)
         make_identity(nc, ident[:])
 
-        x_sb = [keep.tile([P, CHUNK_GROUPS * K_PASS], BF16, name="x_sb%d" % c) for c in range(X_CHUNKS)]
+        x_sb = [keep.tile([P, LOAD_CHUNKS, CHUNK_GROUPS * K_PASS], BF16, name="x_sb%d" % i) for i in range(X_LOADS)]
         x_codes = [
             keep.tile([P, CHUNK_GROUPS * B], U32, name="x_codes%d" % c, align_bytes=64) for c in range(X_CHUNKS)
         ]
@@ -74,6 +76,13 @@ def tile_mylayerfunc_k_kernel(tc, x, weight_words, weight_scales, out):
         for t in range(PLANE_TILES):
             nc.vector.memset(planes[t][:].bitcast(I32), 0)
 
+        half_pi = keep.tile([P, 1], F32)
+        nc.vector.memset(half_pi[:], 0.0)
+        nc.vector.tensor_scalar(out=half_pi[:], in0=half_pi[:], scalar1=0.5 * math.pi, scalar2=None, op0=ALU.add)
+        factor = [keep.tile([P, NACT, C], F32, name="factor%d" % q) for q in range(PIECES)]
+        for q in range(PIECES):
+            nc.vector.memset(factor[q][:], 1.0)
+
         for t in range(PLANE_TILES):
             for quad in range(QUADRANTS):
                 nc.gpsimd.dma_start(
@@ -81,9 +90,9 @@ def tile_mylayerfunc_k_kernel(tc, x, weight_words, weight_scales, out):
                     in_=weight_scales[PLANES * t : PLANES * (t + 1), 4 * quad : 4 * quad + 4, :].bitcast(F32),
                 )
 
-        for c in range(X_CHUNKS):
-            k0 = c * CHUNK_GROUPS * K_PASS
-            nc.sync.dma_start(out=x_sb[c][:], in_=x[:, k0 : k0 + CHUNK_GROUPS * K_PASS])
+        x_loads = x.rearrange("b (i c k) -> i b c k", i=X_LOADS, c=LOAD_CHUNKS)
+        for i in range(X_LOADS):
+            nc.sync.dma_start(out=x_sb[i][:], in_=x_loads[i])
         for g in range(FULL_GROUPS):
             nc.sync.dma_start(
                 out=w_full[g][:].bitcast(I32),
@@ -102,7 +111,7 @@ def tile_mylayerfunc_k_kernel(tc, x, weight_words, weight_scales, out):
         grouped = [None] * X_CHUNKS
 
         def transpose_chunk(c):
-            x_words = x_sb[c][:].bitcast(F32)
+            x_words = x_sb[c // LOAD_CHUNKS][:, c % LOAD_CHUNKS, :].bitcast(F32)
             grouped[c] = stage.tile([P, CHUNK_GROUPS, B, 4], BF16, name="grouped", align_bytes=64)
             for h in range(CHUNK_GROUPS // BANK_GROUPS):
                 xt = psum_t.tile([P, BANK_GROUPS, 2, B], F32, name="xt")
@@ -149,32 +158,39 @@ def tile_mylayerfunc_k_kernel(tc, x, weight_words, weight_scales, out):
 
         def finish_piece(q):
             y = acc[q][:].rearrange("p (c a) -> p a c", a=NACT)
-            arg = tail.tile([P, 4, C], F32, name="arg")
-            nc.vector.tensor_scalar(
-                out=arg[:, 0::3, :], in0=y[:, 1::2, :], scalar1=0.5 * math.pi, scalar2=None, op0=ALU.add
-            )
-            nc.vector.tensor_copy(out=arg[:, 1:3, :], in_=y[:, 2:4, :])
+            y_cos = y[:, 1::2, :]
+            y_sin = y[:, 2:4, :]
             turns = tail.tile([P, 4, C], I32, name="turns")
             nc.vector.tensor_scalar(
-                out=turns[:], in0=arg[:], scalar1=0.5 / math.pi, scalar2=None, op0=ALU.mult
+                out=turns[:, 0:2, :],
+                in0=y_cos,
+                scalar1=0.5 * math.pi,
+                scalar2=0.5 / math.pi,
+                op0=ALU.add,
+                op1=ALU.mult,
+            )
+            nc.vector.tensor_scalar(
+                out=turns[:, 2:4, :], in0=y_sin, scalar1=0.5 / math.pi, scalar2=None, op0=ALU.mult
             )
             reduced = tail.tile([P, 4, C], F32, name="reduced")
             nc.vector.scalar_tensor_tensor(
-                out=reduced[:].rearrange("p a c -> p (a c)"),
-                in0=turns[:].rearrange("p a c -> p (a c)"),
-                scalar=-2.0 * math.pi,
-                in1=arg[:].rearrange("p a c -> p (a c)"),
-                op0=ALU.mult,
-                op1=ALU.add,
+                out=reduced[:, 0:2, :], in0=turns[:, 0:2, :], scalar=-2.0 * math.pi, in1=y_cos, op0=ALU.mult, op1=ALU.add
+            )
+            nc.vector.scalar_tensor_tensor(
+                out=reduced[:, 2:4, :], in0=turns[:, 2:4, :], scalar=-2.0 * math.pi, in1=y_sin, op0=ALU.mult, op1=ALU.add
             )
             res = tail.tile([P, 5, C], F32, name="res")
-            nc.scalar.activation(out=res[:, 1:5, :], in_=reduced[:], func=ACT.Sin)
+            nc.scalar.activation(out=res[:, 1::3, :], in_=reduced[:, 0:2, :], func=ACT.Sin, bias=half_pi[:])
+            nc.scalar.activation(out=res[:, 2:4, :], in_=reduced[:, 2:4, :], func=ACT.Sin)
             nc.vector.tensor_copy(out=res[:, 0, :], in_=y[:, 0, :])
-            inv_cos = tail.tile([P, C], F32, name="inv_cos")
-            nc.vector.reciprocal(out=inv_cos[:], in_=res[:, 4, :])
-            nc.vector.tensor_mul(out=res[:, 3, :], in0=res[:, 3, :], in1=inv_cos[:])
+            nc.vector.reciprocal(out=factor[q][:, 3, :], in_=res[:, 4, :])
             woven = tail.tile([P, C, NACT], F32, name="woven")
-            nc.scalar.copy(out=woven[:], in_=res[:, 0:NACT, :].rearrange("p a c -> p c a"))
+            nc.vector.tensor_tensor(
+                out=woven[:],
+                in0=res[:, 0:NACT, :].rearrange("p a c -> p c a"),
+                in1=factor[q][:].rearrange("p a c -> p c a"),
+                op=ALU.mult,
+            )
             nc.sync.dma_start(
                 out=out[:, q * PIECE : (q + 1) * PIECE], in_=woven[:].rearrange("p c a -> p (c a)")
             )

@@ -39,6 +39,8 @@ TAPER_LOAD = 4
 TAPER_LOADS = TAPER_GROUPS // TAPER_LOAD
 FULL_GROUPS = GROUPS - TAPER_GROUPS
 
+DMA_ALIGN = 256
+
 FLOPS = 2 * B * K * N
 
 
@@ -55,24 +57,27 @@ def tile_mylayerfunc_k_kernel(tc, x, weight_words, weight_scales, out):
         ident = keep.tile([P, P], F32)
         make_identity(nc, ident[:])
 
-        x_sb = [keep.tile([P, LOAD_CHUNKS, CHUNK_GROUPS * K_PASS], BF16, name="x_sb%d" % i) for i in range(X_LOADS)]
+        x_sb = [
+            keep.tile([P, LOAD_CHUNKS, CHUNK_GROUPS * K_PASS], BF16, name="x_sb%d" % i, align_bytes=DMA_ALIGN)
+            for i in range(X_LOADS)
+        ]
         x_codes = [
             keep.tile([P, CHUNK_GROUPS * B], U32, name="x_codes%d" % c, align_bytes=64) for c in range(X_CHUNKS)
         ]
         x_scales = [
             keep.tile([P, CHUNK_GROUPS * B], U8, name="x_scales%d" % c, align_bytes=64) for c in range(X_CHUNKS)
         ]
-        w_full = [keep.tile([P, N], U32, name="w_full%d" % g, align_bytes=64) for g in range(FULL_GROUPS)]
+        w_full = [keep.tile([P, N], U32, name="w_full%d" % g, align_bytes=DMA_ALIGN) for g in range(FULL_GROUPS)]
         w_taper = [
             [
-                keep.tile([P, TAPER_LOAD, PIECE], U32, name="w_taper%d_%d" % (q, h), align_bytes=64)
+                keep.tile([P, TAPER_LOAD, PIECE], U32, name="w_taper%d_%d" % (q, h), align_bytes=DMA_ALIGN)
                 for h in range(TAPER_LOADS)
             ]
             for q in range(PIECES)
         ]
         acc = [psum_y.tile([P, PIECE], F32, name="acc%d" % q) for q in range(PIECES)]
 
-        planes = [keep.tile([P, N], U8, name="planes%d" % t, align_bytes=64) for t in range(PLANE_TILES)]
+        planes = [keep.tile([P, N], U8, name="planes%d" % t, align_bytes=DMA_ALIGN) for t in range(PLANE_TILES)]
         for t in range(PLANE_TILES):
             nc.vector.memset(planes[t][:].bitcast(I32), 0)
 
@@ -184,7 +189,7 @@ def tile_mylayerfunc_k_kernel(tc, x, weight_words, weight_scales, out):
             nc.scalar.activation(out=res[:, 2:4, :], in_=reduced[:, 2:4, :], func=ACT.Sin)
             nc.vector.tensor_copy(out=res[:, 0, :], in_=y[:, 0, :])
             nc.vector.reciprocal(out=factor[q][:, 3, :], in_=res[:, 4, :])
-            woven = tail.tile([P, C, NACT], F32, name="woven")
+            woven = tail.tile([P, C, NACT], F32, name="woven", align_bytes=DMA_ALIGN)
             nc.vector.tensor_tensor(
                 out=woven[:],
                 in0=res[:, 0:NACT, :].rearrange("p a c -> p c a"),

@@ -40,6 +40,11 @@ TAPER_LOADS = TAPER_GROUPS // TAPER_LOAD
 FULL_GROUPS = GROUPS - TAPER_GROUPS
 
 DMA_ALIGN = 256
+LOADS_ALIGN = 4096
+X_BYTES = LOAD_CHUNKS * CHUNK_GROUPS * K_PASS * 2
+W_BYTES = N * 4
+W_OFFSET = X_LOADS * X_BYTES
+PLANES_OFFSET = W_OFFSET + GROUPS * W_BYTES
 
 FLOPS = 2 * B * K * N
 
@@ -48,6 +53,7 @@ def tile_mylayerfunc_k_kernel(tc, x, weight_words, weight_scales, out):
     nc = tc.nc
     with ExitStack() as ctx:
         keep = ctx.enter_context(tc.tile_pool(name="keep", bufs=1))
+        loads = ctx.enter_context(tc.tile_pool(name="loads", bufs=1))
         stage = ctx.enter_context(tc.tile_pool(name="stage", bufs=3))
         tail = ctx.enter_context(tc.tile_pool(name="tail", bufs=PIECES))
         psum_t = ctx.enter_context(tc.psum_pool(name="psum_t", bufs=4))
@@ -58,7 +64,13 @@ def tile_mylayerfunc_k_kernel(tc, x, weight_words, weight_scales, out):
         make_identity(nc, ident[:])
 
         x_sb = [
-            keep.tile([P, LOAD_CHUNKS, CHUNK_GROUPS * K_PASS], BF16, name="x_sb%d" % i, align_bytes=DMA_ALIGN)
+            loads.tile(
+                [P, LOAD_CHUNKS, CHUNK_GROUPS * K_PASS],
+                BF16,
+                name="x_sb%d" % i,
+                align_bytes=LOADS_ALIGN,
+                offset=i * X_BYTES,
+            )
             for i in range(X_LOADS)
         ]
         x_codes = [
@@ -67,17 +79,29 @@ def tile_mylayerfunc_k_kernel(tc, x, weight_words, weight_scales, out):
         x_scales = [
             keep.tile([P, CHUNK_GROUPS * B], U8, name="x_scales%d" % c, align_bytes=64) for c in range(X_CHUNKS)
         ]
-        w_full = [keep.tile([P, N], U32, name="w_full%d" % g, align_bytes=DMA_ALIGN) for g in range(FULL_GROUPS)]
+        w_full = [
+            loads.tile([P, N], U32, name="w_full%d" % g, align_bytes=LOADS_ALIGN, offset=W_OFFSET + g * W_BYTES)
+            for g in range(FULL_GROUPS)
+        ]
         w_taper = [
             [
-                keep.tile([P, TAPER_LOAD, PIECE], U32, name="w_taper%d_%d" % (q, h), align_bytes=DMA_ALIGN)
+                loads.tile(
+                    [P, TAPER_LOAD, PIECE],
+                    U32,
+                    name="w_taper%d_%d" % (q, h),
+                    align_bytes=LOADS_ALIGN,
+                    offset=W_OFFSET + (FULL_GROUPS + q * TAPER_LOADS + h) * W_BYTES,
+                )
                 for h in range(TAPER_LOADS)
             ]
             for q in range(PIECES)
         ]
         acc = [psum_y.tile([P, PIECE], F32, name="acc%d" % q) for q in range(PIECES)]
 
-        planes = [keep.tile([P, N], U8, name="planes%d" % t, align_bytes=DMA_ALIGN) for t in range(PLANE_TILES)]
+        planes = [
+            loads.tile([P, N], U8, name="planes%d" % t, align_bytes=N, offset=PLANES_OFFSET + t * N)
+            for t in range(PLANE_TILES)
+        ]
         for t in range(PLANE_TILES):
             nc.vector.memset(planes[t][:].bitcast(I32), 0)
 

import math
from contextlib import ExitStack

import concourse.mybir as mybir
from concourse.masks import make_identity

F32 = mybir.dt.float32
BF16 = mybir.dt.bfloat16
I32 = mybir.dt.int32
U32 = mybir.dt.uint32
U8 = mybir.dt.uint8
FP8X4 = mybir.dt.float8_e4m3fn_x4
ALU = mybir.AluOpType
ACT = mybir.ActivationFunctionType

P = 128
B, K, N = 128, 16384, 1024
K_PASS = 512
GROUPS = K // K_PASS
PAIRS = K_PASS // 2

CHUNK_GROUPS = 4
X_CHUNKS = GROUPS // CHUNK_GROUPS
LOAD_CHUNKS = 2
X_LOADS = X_CHUNKS // LOAD_CHUNKS
BANK_GROUPS = 2

PIECES = 4
PIECE = N // PIECES
NACT = 4
C = PIECE // NACT

PLANES = 4
PLANE_TILES = GROUPS // PLANES
QUADRANTS = 4

TAPER_GROUPS = 8
TAPER_LOAD = 4
TAPER_LOADS = TAPER_GROUPS // TAPER_LOAD
FULL_GROUPS = GROUPS - TAPER_GROUPS

DMA_ALIGN = 256
LOADS_ALIGN = 4096
X_BYTES = LOAD_CHUNKS * CHUNK_GROUPS * K_PASS * 2
W_BYTES = N * 4
W_OFFSET = X_LOADS * X_BYTES
PLANES_OFFSET = W_OFFSET + GROUPS * W_BYTES

FLOPS = 2 * B * K * N


def tile_mylayerfunc_k_kernel(tc, x, weight_words, weight_scales, out):
    nc = tc.nc
    with ExitStack() as ctx:
        keep = ctx.enter_context(tc.tile_pool(name="keep", bufs=1))
        loads = ctx.enter_context(tc.tile_pool(name="loads", bufs=1))
        stage = ctx.enter_context(tc.tile_pool(name="stage", bufs=3))
        tail = ctx.enter_context(tc.tile_pool(name="tail", bufs=PIECES))
        psum_t = ctx.enter_context(tc.psum_pool(name="psum_t", bufs=4))
        psum_y = ctx.enter_context(tc.psum_pool(name="psum_y", bufs=1))
        ctx.enter_context(tc.manual_schedule())

        ident = keep.tile([P, P], F32)
        make_identity(nc, ident[:])

        x_sb = [
            loads.tile(
                [P, LOAD_CHUNKS, CHUNK_GROUPS * K_PASS],
                BF16,
                name="x_sb%d" % i,
                align_bytes=LOADS_ALIGN,
                offset=i * X_BYTES,
            )
            for i in range(X_LOADS)
        ]
        x_codes = [
            keep.tile([P, CHUNK_GROUPS * B], U32, name="x_codes%d" % c, align_bytes=64) for c in range(X_CHUNKS)
        ]
        x_scales = [
            keep.tile([P, CHUNK_GROUPS * B], U8, name="x_scales%d" % c, align_bytes=64) for c in range(X_CHUNKS)
        ]
        w_full = [
            loads.tile([P, N], U32, name="w_full%d" % g, align_bytes=LOADS_ALIGN, offset=W_OFFSET + g * W_BYTES)
            for g in range(FULL_GROUPS)
        ]
        w_taper = [
            [
                loads.tile(
                    [P, TAPER_LOAD, PIECE],
                    U32,
                    name="w_taper%d_%d" % (q, h),
                    align_bytes=LOADS_ALIGN,
                    offset=W_OFFSET + (FULL_GROUPS + q * TAPER_LOADS + h) * W_BYTES,
                )
                for h in range(TAPER_LOADS)
            ]
            for q in range(PIECES)
        ]
        acc = [psum_y.tile([P, PIECE], F32, name="acc%d" % q) for q in range(PIECES)]

        planes = [
            loads.tile([P, N], U8, name="planes%d" % t, align_bytes=N, offset=PLANES_OFFSET + t * N)
            for t in range(PLANE_TILES)
        ]
        for t in range(PLANE_TILES):
            nc.vector.memset(planes[t][:].bitcast(I32), 0)

        half_pi = keep.tile([P, 1], F32)
        nc.vector.memset(half_pi[:], 0.0)
        nc.vector.tensor_scalar(out=half_pi[:], in0=half_pi[:], scalar1=0.5 * math.pi, scalar2=None, op0=ALU.add)
        factor = [keep.tile([P, NACT, C], F32, name="factor%d" % q) for q in range(PIECES)]
        for q in range(PIECES):
            nc.vector.memset(factor[q][:], 1.0)

        for t in range(PLANE_TILES):
            for quad in range(QUADRANTS):
                nc.gpsimd.dma_start(
                    out=planes[t][32 * quad : 32 * quad + 4 * PLANES, :].bitcast(F32),
                    in_=weight_scales[PLANES * t : PLANES * (t + 1), 4 * quad : 4 * quad + 4, :].bitcast(F32),
                )

        x_loads = x.rearrange("b (i c k) -> i b c k", i=X_LOADS, c=LOAD_CHUNKS)
        for i in range(X_LOADS):
            nc.sync.dma_start(out=x_sb[i][:], in_=x_loads[i])
        for g in range(FULL_GROUPS):
            nc.sync.dma_start(
                out=w_full[g][:].bitcast(I32),
                in_=weight_words[g].rearrange("p n t -> p (n t)").bitcast(I32),
            )
        for q in range(PIECES):
            for h in range(TAPER_LOADS):
                g0 = FULL_GROUPS + h * TAPER_LOAD
                nc.sync.dma_start(
                    out=w_taper[q][h][:].bitcast(I32),
                    in_=weight_words[g0 : g0 + TAPER_LOAD, :, q * PIECE : (q + 1) * PIECE, :]
                    .rearrange("g p n t -> p g (n t)")
                    .bitcast(I32),
                )

        grouped = [None] * X_CHUNKS

        def transpose_chunk(c):
            x_words = x_sb[c // LOAD_CHUNKS][:, c % LOAD_CHUNKS, :].bitcast(F32)
            grouped[c] = stage.tile([P, CHUNK_GROUPS, B, 4], BF16, name="grouped", align_bytes=64)
            for h in range(CHUNK_GROUPS // BANK_GROUPS):
                xt = psum_t.tile([P, BANK_GROUPS, 2, B], F32, name="xt")
                for gi in range(BANK_GROUPS):
                    w0 = (h * BANK_GROUPS + gi) * PAIRS
                    for u in range(2):
                        nc.tensor.transpose(xt[:, gi, u, :], x_words[:, w0 + u : w0 + PAIRS : 2], ident[:])
                dst = grouped[c][:, h * BANK_GROUPS : (h + 1) * BANK_GROUPS, :, :].bitcast(F32)
                src = xt[:].rearrange("p g u b -> p g b u")
                if h % 2 == 0:
                    nc.vector.tensor_copy(out=dst, in_=src)
                else:
                    nc.scalar.copy(out=dst, in_=src)

        def quantise_chunk(c):
            nc.vector.quantize_mx(
                out=x_codes[c][:].bitcast(FP8X4),
                scales=x_scales[c][:],
                in_=grouped[c][:].rearrange("p g b t -> p (g b t)"),
            )

        for c in range(X_CHUNKS):
            transpose_chunk(c)
            if c > 0:
                quantise_chunk(c - 1)
        quantise_chunk(X_CHUNKS - 1)

        def mx_pass(g, q, w_cols):
            c, gi = divmod(g, CHUNK_GROUPS)
            t, j = divmod(g, PLANES)
            nc.tensor.matmul_mx(
                out=acc[q][:],
                lhsT=x_codes[c][:, gi * B : (gi + 1) * B].bitcast(FP8X4),
                lhsT_scale=x_scales[c][:, gi * B : (gi + 1) * B],
                rhs=w_cols.bitcast(FP8X4),
                rhs_scale=planes[t][4 * j : P, q * PIECE : (q + 1) * PIECE],
                start=(g == 0),
                stop=(g == GROUPS - 1),
            )

        for g in range(FULL_GROUPS):
            for q in range(PIECES):
                mx_pass(g, q, w_full[g][:, q * PIECE : (q + 1) * PIECE])

        def finish_piece(q):
            y = acc[q][:].rearrange("p (c a) -> p a c", a=NACT)
            y_cos = y[:, 1::2, :]
            y_sin = y[:, 2:4, :]
            turns = tail.tile([P, 4, C], I32, name="turns")
            nc.vector.tensor_scalar(
                out=turns[:, 0:2, :],
                in0=y_cos,
                scalar1=0.5 * math.pi,
                scalar2=0.5 / math.pi,
                op0=ALU.add,
                op1=ALU.mult,
            )
            nc.vector.tensor_scalar(
                out=turns[:, 2:4, :], in0=y_sin, scalar1=0.5 / math.pi, scalar2=None, op0=ALU.mult
            )
            reduced = tail.tile([P, 4, C], F32, name="reduced")
            nc.vector.scalar_tensor_tensor(
                out=reduced[:, 0:2, :], in0=turns[:, 0:2, :], scalar=-2.0 * math.pi, in1=y_cos, op0=ALU.mult, op1=ALU.add
            )
            nc.vector.scalar_tensor_tensor(
                out=reduced[:, 2:4, :], in0=turns[:, 2:4, :], scalar=-2.0 * math.pi, in1=y_sin, op0=ALU.mult, op1=ALU.add
            )
            res = tail.tile([P, 5, C], F32, name="res")
            nc.scalar.activation(out=res[:, 1::3, :], in_=reduced[:, 0:2, :], func=ACT.Sin, bias=half_pi[:])
            nc.scalar.activation(out=res[:, 2:4, :], in_=reduced[:, 2:4, :], func=ACT.Sin)
            nc.vector.tensor_copy(out=res[:, 0, :], in_=y[:, 0, :])
            nc.vector.reciprocal(out=factor[q][:, 3, :], in_=res[:, 4, :])
            woven = tail.tile([P, C, NACT], F32, name="woven", align_bytes=DMA_ALIGN)
            nc.vector.tensor_tensor(
                out=woven[:],
                in0=res[:, 0:NACT, :].rearrange("p a c -> p c a"),
                in1=factor[q][:].rearrange("p a c -> p c a"),
                op=ALU.mult,
            )
            nc.sync.dma_start(
                out=out[:, q * PIECE : (q + 1) * PIECE], in_=woven[:].rearrange("p c a -> p (c a)")
            )

        for q in range(PIECES):
            for h in range(TAPER_LOADS):
                for gi in range(TAPER_LOAD):
                    mx_pass(FULL_GROUPS + h * TAPER_LOAD + gi, q, w_taper[q][h][:, gi, :])
            finish_piece(q)
